import numpy as np
import ml_dtypes


def mxq(x, axis, fmt="e4m3"):
    dtype, down = {"e4m3": (ml_dtypes.float8_e4m3fn, 7), "e5m2": (ml_dtypes.float8_e5m2, 14)}[fmt]
    v = np.moveaxis(np.asarray(x, np.float32).astype(ml_dtypes.bfloat16).astype(np.float64), axis, -1)
    blocks = v.reshape(v.shape[:-1] + (-1, 32))
    amax = np.abs(blocks).max(-1, keepdims=True)
    byte = np.maximum(np.where(amax > 0, np.frexp(amax)[1] - 1 + 127, 0) - down, 1)
    scale = np.exp2(byte - 127.0)
    codes = (blocks / scale).astype(np.float32).astype(dtype).astype(np.float64)
    return np.moveaxis((codes * scale).reshape(v.shape), -1, axis)


WIDE = False


def mx_kscale(k):
    if not WIDE:
        return np.ones(k)
    levels = np.array([10, -10, 5, -5, 0])
    a = np.random.permutation(np.resize(levels, k // 512 * 4)).reshape(k // 512, 4)
    idx = np.arange(k)
    return np.exp2(a[idx // 512, idx % 128 // 32])


BF16 = ml_dtypes.bfloat16


def bf(x):
    return np.asarray(x, np.float32).astype(BF16)


def f64(x):
    return np.asarray(x).astype(np.float64)


B, S, DIM, HEADS = 1, 4096, 512, 4
HD = DIM // HEADS
EPS = 1e-6


def rms_norm(x, g):
    var = np.mean(np.square(x), axis=-1, keepdims=True)
    return x * (1.0 / np.sqrt(var + EPS)) * g


def rope(x, cos, sin):
    x1, x2 = np.split(x, 2, axis=-1)
    rot = np.concatenate([-x2, x1], axis=-1)
    return x * cos[None, :, None, :] + rot * sin[None, :, None, :]


def setup_inputs():
    s = mx_kscale(DIM)
    return {
        "hidden_states": bf(np.random.standard_normal((B, S, DIM)) * s),
        "cos": bf(np.random.uniform(-1.0, 1.0, (S, HD))),
        "sin": bf(np.random.uniform(-1.0, 1.0, (S, HD))),
        "w_qk": bf(np.random.standard_normal((DIM + DIM, DIM)) / np.sqrt(DIM) / s[None, :]),
        "b_qk": bf(np.random.standard_normal(DIM + DIM) * 0.2),
        "g_q": bf(1.0 + 0.1 * np.random.standard_normal(DIM)),
        "g_k": bf(1.0 + 0.1 * np.random.standard_normal(DIM)),
    }


def reference(hidden_states, cos, sin, w_qk, b_qk, g_q, g_k):
    c, sn = f64(cos), f64(sin)
    qk = (mxq(f64(hidden_states), 2, "e4m3") @ mxq(f64(w_qk), 1, "e4m3").T) + f64(b_qk)
    q = rms_norm(qk[:, :, :DIM], f64(g_q)).reshape(B, S, HEADS, HD)
    k = rms_norm(qk[:, :, DIM:], f64(g_k)).reshape(B, S, HEADS, HD)
    return rope(q, c, sn), rope(k, c, sn)

@@ -1,0 +1,337 @@
+from contextlib import ExitStack
+
+import concourse.mybir as mybir
+from concourse.masks import make_identity
+
+F32 = mybir.dt.float32
+BF16 = mybir.dt.bfloat16
+U32 = mybir.dt.uint32
+U8 = mybir.dt.uint8
+FP8X4 = mybir.dt.float8_e4m3fn_x4
+ACT = mybir.ActivationFunctionType
+ALU = mybir.AluOpType
+
+P = 128
+TOKENS = 4096
+DIM = 512
+HEAD = 128
+HALF = HEAD // 2
+HEADS = DIM // HEAD
+SIDES = 2
+WORDS = DIM // 2
+TILES = TOKENS // P
+GROUP = 4
+GROUPS = TILES // GROUP
+GROUP_TOKENS = GROUP * P
+UNITS = GROUPS * SIDES
+STEPS = 2 * UNITS
+EPS = 1e-6
+
+FLOPS = 2 * TOKENS * SIDES * DIM * DIM
+
+
+def turn_two_blocks(nc, bank, ident, two_blocks):
+    for blk in range(2):
+        for u in range(2):
+            nc.tensor.transpose(bank[:, blk, u, :], two_blocks[:, blk, u * P : (u + 1) * P], ident)
+
+
+def copy_two_blocks(nc, bank, grouped, on_scalar):
+    planes = bank[:].rearrange("p b u r -> p b r u")
+    if on_scalar:
+        nc.scalar.copy(out=grouped, in_=planes)
+    else:
+        nc.vector.tensor_copy(out=grouped, in_=planes)
+
+
+def tile_dynamicselfattention_pa_t_kernel(
+    tc, hidden_states, cos, sin, w_qk, b_qk, g_q, g_k, out_0, out_1
+):
+    nc = tc.nc
+    h_dram = hidden_states.flatten_outer_dims().rearrange("(p T) k -> p T k", T=TILES)
+    cos_dram = cos.rearrange("(p T) d -> p T d", T=TILES)
+    sin_dram = sin.rearrange("(p T) d -> p T d", T=TILES)
+    w_dram = w_qk.rearrange("(j p) k -> p j k", p=P)
+    out_dram = [
+        o.flatten_outer_dims().rearrange("(p T h) d -> p T (h d)", T=TILES, h=HEADS)
+        for o in (out_0, out_1)
+    ]
+
+    with ExitStack() as stack:
+        stack.enter_context(tc.manual_schedule())
+        keep = stack.enter_context(tc.tile_pool(name="keep", bufs=1))
+        quant = stack.enter_context(tc.tile_pool(name="quant", bufs=2))
+        zt_pool = stack.enter_context(tc.tile_pool(name="zt_pool", bufs=12))
+        ysq_pool = stack.enter_context(tc.tile_pool(name="ysq_pool", bufs=10))
+        small = stack.enter_context(tc.tile_pool(name="small", bufs=4))
+        cos_pool = stack.enter_context(tc.tile_pool(name="cos_pool", bufs=4))
+        sin_pool = stack.enter_context(tc.tile_pool(name="sin_pool", bufs=3))
+        turn_pool = stack.enter_context(tc.psum_pool(name="turn_pool", bufs=1))
+        acc_pool = stack.enter_context(tc.psum_pool(name="acc_pool", bufs=3))
+        z_pool = stack.enter_context(tc.psum_pool(name="z_pool", bufs=3))
+        ss_pool = stack.enter_context(tc.psum_pool(name="ss_pool", bufs=1))
+
+        eps = keep.tile([P, 1], F32)
+        nc.vector.memset(eps[:], EPS)
+        warm = keep.tile([P, 1], F32)
+        nc.scalar.activation(out=warm[:], in_=eps[:], func=ACT.Sqrt)
+        ones = keep.tile([P, 1], F32)
+        nc.vector.memset(ones[:], 1.0)
+        vec_rows = keep.tile([P, P], BF16)
+        nc.vector.memset(vec_rows[:], 0.0)
+        ident = keep.tile([P, P], F32)
+        make_identity(nc, ident[:])
+
+        w_sb = keep.tile([P, SIDES * HEADS * DIM], BF16)
+        w_rows = w_sb[:].rearrange("p (j k) -> p j k", k=DIM)
+        h_sb = keep.tile([P, TILES * DIM], BF16)
+        h_rows = h_sb[:].rearrange("p (T k) -> p T k", k=DIM)
+
+        def load_w(pair):
+            two = slice(2 * pair, 2 * pair + 2)
+            nc.sync.dma_start(out=w_rows[:, two, :], in_=w_dram[:, two, :])
+
+        def load_h(g):
+            four = slice(g * GROUP, (g + 1) * GROUP)
+            nc.sync.dma_start(out=h_rows[:, four, :], in_=h_dram[:, four, :])
+
+        nc.scalar.dma_start(out=vec_rows[0:8, :], in_=b_qk.rearrange("(j d) -> j d", d=HEAD))
+        nc.scalar.dma_start(out=vec_rows[8:12, :], in_=g_q.rearrange("(j d) -> j d", d=HEAD))
+        nc.scalar.dma_start(out=vec_rows[12:16, :], in_=g_k.rearrange("(j d) -> j d", d=HEAD))
+        load_w(0)
+        load_h(0)
+        for pair in range(1, SIDES * HEADS // 2):
+            load_w(pair)
+        load_h(1)
+        cos_sb = keep.tile([P, TILES, HEAD], BF16)
+        nc.sync.dma_start(out=cos_sb[:], in_=cos_dram)
+        sin_swap = keep.tile([P, TILES, HEAD], BF16)
+        nc.sync.dma_start(out=sin_swap[:, :, 0:HALF], in_=sin_dram[:, :, HALF:HEAD])
+        nc.sync.dma_start(out=sin_swap[:, :, HALF:HEAD], in_=sin_dram[:, :, 0:HALF])
+        for g in range(2, GROUPS):
+            load_h(g)
+
+        w_words = w_sb[:].bitcast(F32).rearrange("p (j w) -> p j w", w=WORDS)
+        h_words = h_sb[:].bitcast(F32).rearrange("p (T w) -> p T w", w=WORDS)
+        w_grouped = keep.tile([P, SIDES * DIM * 4], BF16, align_bytes=64)
+        w_grouped_words = w_grouped[:].bitcast(F32).rearrange("p (j r u) -> p j r u", r=P, u=2)
+        w_codes = keep.tile([P, SIDES * DIM], U32, align_bytes=64)
+        w_scales = keep.tile([P, SIDES * DIM], U8, align_bytes=64)
+        h_grouped = {}
+        h_codes = {}
+        h_scales = {}
+        h_bank = {}
+
+        def turn_weights(pair):
+            bank = z_pool.tile([P, 2, 2, P], F32, tag="z")
+            two = slice(2 * pair, 2 * pair + 2)
+            turn_two_blocks(nc, bank, ident[:], w_words[:, two, :])
+            copy_two_blocks(nc, bank, w_grouped_words[:, two], False)
+
+        def quantise_weights(pair):
+            nc.vector.quantize_mx(
+                out=w_codes[:, 2 * P * pair : 2 * P * (pair + 1)].bitcast(FP8X4),
+                scales=w_scales[:, 2 * P * pair : 2 * P * (pair + 1)],
+                in_=w_grouped[:, 8 * P * pair : 8 * P * (pair + 1)],
+            )
+
+        def turn_hidden(g, pair, pool, tag):
+            if pair == 0:
+                h_grouped[g] = quant.tile([P, GROUP_TOKENS * 4], BF16, align_bytes=64, name="h_grouped")
+            first = g * GROUP + 2 * pair
+            h_bank[g, pair] = pool.tile([P, 2, 2, P], F32, tag=tag, name="h_bank")
+            turn_two_blocks(nc, h_bank[g, pair], ident[:], h_words[:, first : first + 2, :])
+
+        def copy_hidden(g, pair):
+            words = h_grouped[g][:].bitcast(F32).rearrange("p (t r u) -> p t r u", r=P, u=2)
+            copy_two_blocks(nc, h_bank[g, pair], words[:, 2 * pair : 2 * pair + 2], pair == 1)
+
+        def quantise_hidden(g):
+            h_codes[g] = quant.tile([P, GROUP_TOKENS], U32, align_bytes=64, name="h_codes")
+            h_scales[g] = quant.tile([P, GROUP_TOKENS], U8, align_bytes=64, name="h_scales")
+            nc.vector.quantize_mx(
+                out=h_codes[g][:].bitcast(FP8X4), scales=h_scales[g][:], in_=h_grouped[g][:]
+            )
+
+        turn_weights(0)
+        turn_hidden(0, 0, z_pool, "z")
+        copy_hidden(0, 0)
+        turn_hidden(0, 1, z_pool, "z")
+        copy_hidden(0, 1)
+        quantise_weights(0)
+
+        vec_f32 = keep.tile([P, P], F32)
+        nc.vector.tensor_copy(out=vec_f32[:], in_=vec_rows[:])
+        vec_ps = turn_pool.tile([P, P], F32, tag="turn")
+        nc.tensor.transpose(vec_ps[:], vec_f32[:], ident[:])
+        cols = keep.tile([P, 16], F32)
+        nc.vector.tensor_copy(out=cols[:], in_=vec_ps[:, 0:16])
+        bias_col = cols[:, 0:8]
+        gain_col = cols[:, 8:16]
+        gain_bias = keep.tile([P, 8], F32)
+        nc.vector.tensor_mul(out=gain_bias[:], in0=bias_col, in1=gain_col)
+        quantise_hidden(0)
+
+        acc = {}
+        zt = {}
+        ysq = {}
+        ss = {}
+        std = {}
+        rstd = {}
+        z = {}
+        with_cos = {}
+        with_sin = {}
+
+        def project(s):
+            if s < 0 or s >= STEPS:
+                return
+            unit = s // 2
+            for i in range(2):
+                j = (unit % SIDES) * HEADS + 2 * (s % 2) + i
+                w_cols = slice(j * P, (j + 1) * P)
+                acc[s, i] = acc_pool.tile([P, GROUP_TOKENS], F32, name="acc")
+                nc.tensor.matmul_mx(
+                    out=acc[s, i][:],
+                    lhsT=w_codes[:, w_cols].bitcast(FP8X4),
+                    lhsT_scale=w_scales[:, w_cols],
+                    rhs=h_codes[unit // SIDES][:].bitcast(FP8X4),
+                    rhs_scale=h_scales[unit // SIDES][:],
+                    start=True,
+                    stop=True,
+                )
+
+        def scale_and_square(s):
+            if s < 0 or s >= STEPS:
+                return
+            unit = s // 2
+            for i in range(2):
+                head = 2 * (s % 2) + i
+                j = (unit % SIDES) * HEADS + head
+                zt[unit, head] = zt_pool.tile([P, GROUP_TOKENS], F32, name="zt")
+                nc.scalar.activation(
+                    out=zt[unit, head][:],
+                    in_=acc[s, i][:],
+                    func=ACT.Identity,
+                    bias=gain_bias[:, j : j + 1],
+                    scale=gain_col[:, j : j + 1],
+                )
+                ysq[unit, head] = ysq_pool.tile([P, GROUP_TOKENS], F32, name="ysq")
+                nc.scalar.activation(
+                    out=ysq[unit, head][:],
+                    in_=acc[s, i][:],
+                    func=ACT.Square,
+                    bias=bias_col[:, j : j + 1],
+                )
+
+        def sum_squares(s):
+            if s < 0 or s >= STEPS:
+                return
+            unit = s // 2
+            if s % 2 == 0:
+                ss[unit] = ss_pool.tile([P, GROUP], F32, name="ss")
+            for i in range(2):
+                t = 2 * (s % 2) + i
+                for head in range(HEADS):
+                    nc.tensor.matmul(
+                        out=ss[unit][:, t : t + 1],
+                        lhsT=ysq[unit, head][:, t * P : (t + 1) * P],
+                        rhs=ones[:],
+                        start=(head == 0),
+                        stop=(head == HEADS - 1),
+                    )
+
+        def root(unit):
+            if unit < 0 or unit >= UNITS:
+                return
+            std[unit] = small.tile([P, GROUP], F32, name="std")
+            nc.scalar.activation(
+                out=std[unit][:], in_=ss[unit][:], func=ACT.Sqrt, bias=eps[:], scale=1.0 / DIM
+            )
+
+        def invert(unit):
+            if unit < 0 or unit >= UNITS:
+                return
+            rstd[unit] = small.tile([P, GROUP], F32, name="rstd")
+            nc.vector.reciprocal(out=rstd[unit][:], in_=std[unit][:])
+
+        def turn_back(s, i):
+            if s < 0 or s >= STEPS:
+                return
+            unit = s // 2
+            t = 2 * (s % 2) + i
+            z[s, i] = z_pool.tile([P, HEADS, HEAD], F32, tag="z", name="z")
+            for head in range(HEADS):
+                nc.tensor.transpose(
+                    z[s, i][:, head, :], zt[unit, head][:, t * P : (t + 1) * P], ident[:]
+                )
+
+        def rotate(s):
+            if s < 0 or s >= STEPS:
+                return
+            unit = s // 2
+            if s % 2 == 0:
+                with_cos[unit] = cos_pool.tile([P, GROUP, DIM], F32, name="with_cos")
+                with_sin[unit] = sin_pool.tile([P, GROUP, DIM], F32, name="with_sin")
+            for i in range(2):
+                t = 2 * (s % 2) + i
+                T = (unit // SIDES) * GROUP + t
+                for table, product in ((cos_sb, with_cos[unit]), (sin_swap, with_sin[unit])):
+                    nc.vector.scalar_tensor_tensor(
+                        out=product[:, t, :].rearrange("p (h d) -> p h d", d=HEAD),
+                        in0=z[s, i][:],
+                        scalar=rstd[unit][:, t : t + 1],
+                        in1=table[:, T, :].unsqueeze(1).to_broadcast([P, HEADS, HEAD]),
+                        op0=ALU.mult,
+                        op1=ALU.mult,
+                    )
+
+        def combine_store(unit):
+            if unit < 0 or unit >= UNITS:
+                return
+            c_halves = with_cos[unit][:].rearrange("p t (h x d) -> p (t h) x d", x=2, d=HALF)
+            s_halves = with_sin[unit][:].rearrange("p t (h x d) -> p (t h) x d", x=2, d=HALF)
+            nc.gpsimd.tensor_tensor(
+                out=c_halves[:, :, 0, :],
+                in0=c_halves[:, :, 0, :],
+                in1=s_halves[:, :, 1, :],
+                op=ALU.subtract,
+            )
+            nc.gpsimd.tensor_tensor(
+                out=c_halves[:, :, 1, :],
+                in0=c_halves[:, :, 1, :],
+                in1=s_halves[:, :, 0, :],
+                op=ALU.add,
+            )
+            g = unit // SIDES
+            nc.sync.dma_start(
+                out=out_dram[unit % SIDES][:, g * GROUP : (g + 1) * GROUP, :],
+                in_=with_cos[unit][:],
+            )
+
+        for k in range(-1, STEPS + 5):
+            next_group = k // 4 + 1
+            phase = k % 4
+            prepare = k >= 0 and next_group < GROUPS
+            turn_back(k - 3, 0)
+            sum_squares(k - 2)
+            if prepare and phase < 2:
+                turn_hidden(next_group, phase, turn_pool, "turn")
+            project(k + 1)
+            turn_back(k - 3, 1)
+            scale_and_square(k)
+            if prepare and phase == 1:
+                copy_hidden(next_group, 1)
+            if k % 2 == 1:
+                root((k - 3) // 2)
+            if k % 2 == 0:
+                invert((k - 4) // 2)
+            rotate(k - 4)
+            if prepare and phase == 0:
+                copy_hidden(next_group, 0)
+            if prepare and phase == 2:
+                quantise_hidden(next_group)
+            if k + 2 < SIDES * HEADS // 2:
+                turn_weights(k + 2)
+                quantise_weights(k + 2)
+            if k % 2 == 0:
+                combine_store((k - 6) // 2)

@@ -61,22 +61,18 @@ def tile_dynamicselfattention_pa_t_kernel(
         stack.enter_context(tc.manual_schedule())
         keep = stack.enter_context(tc.tile_pool(name="keep", bufs=1))
         quant = stack.enter_context(tc.tile_pool(name="quant", bufs=2))
-        zt_pool = stack.enter_context(tc.tile_pool(name="zt_pool", bufs=12))
-        ysq_pool = stack.enter_context(tc.tile_pool(name="ysq_pool", bufs=10))
+        zt_pool = stack.enter_context(tc.tile_pool(name="zt_pool", bufs=14))
+        ysq_pool = stack.enter_context(tc.tile_pool(name="ysq_pool", bufs=12))
         small = stack.enter_context(tc.tile_pool(name="small", bufs=4))
         cos_pool = stack.enter_context(tc.tile_pool(name="cos_pool", bufs=4))
         sin_pool = stack.enter_context(tc.tile_pool(name="sin_pool", bufs=3))
-        turn_pool = stack.enter_context(tc.psum_pool(name="turn_pool", bufs=1))
-        acc_pool = stack.enter_context(tc.psum_pool(name="acc_pool", bufs=3))
-        z_pool = stack.enter_context(tc.psum_pool(name="z_pool", bufs=3))
-        ss_pool = stack.enter_context(tc.psum_pool(name="ss_pool", bufs=1))
+        bank_pool = stack.enter_context(tc.psum_pool(name="bank_pool", bufs=6))
+        ss_pool = stack.enter_context(tc.psum_pool(name="ss_pool", bufs=2))
 
         eps = keep.tile([P, 1], F32)
         nc.vector.memset(eps[:], EPS)
         warm = keep.tile([P, 1], F32)
         nc.scalar.activation(out=warm[:], in_=eps[:], func=ACT.Sqrt)
-        ones = keep.tile([P, 1], F32)
-        nc.vector.memset(ones[:], 1.0)
         vec_rows = keep.tile([P, P], BF16)
         nc.vector.memset(vec_rows[:], 0.0)
         ident = keep.tile([P, P], F32)
@@ -102,14 +98,15 @@ def tile_dynamicselfattention_pa_t_kernel(
         load_h(0)
         for pair in range(1, SIDES * HEADS // 2):
             load_w(pair)
-        load_h(1)
         cos_sb = keep.tile([P, TILES, HEAD], BF16)
-        nc.sync.dma_start(out=cos_sb[:], in_=cos_dram)
         sin_swap = keep.tile([P, TILES, HEAD], BF16)
-        nc.sync.dma_start(out=sin_swap[:, :, 0:HALF], in_=sin_dram[:, :, HALF:HEAD])
-        nc.sync.dma_start(out=sin_swap[:, :, HALF:HEAD], in_=sin_dram[:, :, 0:HALF])
-        for g in range(2, GROUPS):
-            load_h(g)
+        for part in range(2):
+            for g in range(max(1, part * GROUPS // 2), (part + 1) * GROUPS // 2):
+                load_h(g)
+            some = slice(part * TILES // 2, (part + 1) * TILES // 2)
+            nc.sync.dma_start(out=cos_sb[:, some, :], in_=cos_dram[:, some, :])
+            nc.sync.dma_start(out=sin_swap[:, some, 0:HALF], in_=sin_dram[:, some, HALF:HEAD])
+            nc.sync.dma_start(out=sin_swap[:, some, HALF:HEAD], in_=sin_dram[:, some, 0:HALF])
 
         w_words = w_sb[:].bitcast(F32).rearrange("p (j w) -> p j w", w=WORDS)
         h_words = h_sb[:].bitcast(F32).rearrange("p (T w) -> p T w", w=WORDS)
@@ -117,13 +114,12 @@ def tile_dynamicselfattention_pa_t_kernel(
         w_grouped_words = w_grouped[:].bitcast(F32).rearrange("p (j r u) -> p j r u", r=P, u=2)
         w_codes = keep.tile([P, SIDES * DIM], U32, align_bytes=64)
         w_scales = keep.tile([P, SIDES * DIM], U8, align_bytes=64)
+        h_codes = keep.tile([P, TOKENS], U32, align_bytes=64)
+        h_scales = keep.tile([P, TOKENS], U8, align_bytes=64)
         h_grouped = {}
-        h_codes = {}
-        h_scales = {}
-        h_bank = {}
 
         def turn_weights(pair):
-            bank = z_pool.tile([P, 2, 2, P], F32, tag="z")
+            bank = bank_pool.tile([P, 2, 2, P], F32, tag="bank")
             two = slice(2 * pair, 2 * pair + 2)
             turn_two_blocks(nc, bank, ident[:], w_words[:, two, :])
             copy_two_blocks(nc, bank, w_grouped_words[:, two], False)
@@ -135,34 +131,30 @@ def tile_dynamicselfattention_pa_t_kernel(
                 in_=w_grouped[:, 8 * P * pair : 8 * P * (pair + 1)],
             )
 
-        def turn_hidden(g, pair, pool, tag):
-            if pair == 0:
-                h_grouped[g] = quant.tile([P, GROUP_TOKENS * 4], BF16, align_bytes=64, name="h_grouped")
-            first = g * GROUP + 2 * pair
-            h_bank[g, pair] = pool.tile([P, 2, 2, P], F32, tag=tag, name="h_bank")
-            turn_two_blocks(nc, h_bank[g, pair], ident[:], h_words[:, first : first + 2, :])
-
-        def copy_hidden(g, pair):
+        def turn_hidden(g, second_on_scalar):
+            h_grouped[g] = quant.tile([P, GROUP_TOKENS * 4], BF16, align_bytes=64, name="h_grouped")
             words = h_grouped[g][:].bitcast(F32).rearrange("p (t r u) -> p t r u", r=P, u=2)
-            copy_two_blocks(nc, h_bank[g, pair], words[:, 2 * pair : 2 * pair + 2], pair == 1)
+            for pair in range(GROUP // 2):
+                first = g * GROUP + 2 * pair
+                bank = bank_pool.tile([P, 2, 2, P], F32, tag="bank")
+                turn_two_blocks(nc, bank, ident[:], h_words[:, first : first + 2, :])
+                copy_two_blocks(
+                    nc, bank, words[:, 2 * pair : 2 * pair + 2], second_on_scalar and pair == 1
+                )
 
         def quantise_hidden(g):
-            h_codes[g] = quant.tile([P, GROUP_TOKENS], U32, align_bytes=64, name="h_codes")
-            h_scales[g] = quant.tile([P, GROUP_TOKENS], U8, align_bytes=64, name="h_scales")
+            tokens = slice(g * GROUP_TOKENS, (g + 1) * GROUP_TOKENS)
             nc.vector.quantize_mx(
-                out=h_codes[g][:].bitcast(FP8X4), scales=h_scales[g][:], in_=h_grouped[g][:]
+                out=h_codes[:, tokens].bitcast(FP8X4), scales=h_scales[:, tokens], in_=h_grouped[g][:]
             )
 
         turn_weights(0)
-        turn_hidden(0, 0, z_pool, "z")
-        copy_hidden(0, 0)
-        turn_hidden(0, 1, z_pool, "z")
-        copy_hidden(0, 1)
+        turn_hidden(0, True)
         quantise_weights(0)
 
         vec_f32 = keep.tile([P, P], F32)
         nc.vector.tensor_copy(out=vec_f32[:], in_=vec_rows[:])
-        vec_ps = turn_pool.tile([P, P], F32, tag="turn")
+        vec_ps = bank_pool.tile([P, P], F32, tag="bank")
         nc.tensor.transpose(vec_ps[:], vec_f32[:], ident[:])
         cols = keep.tile([P, 16], F32)
         nc.vector.tensor_copy(out=cols[:], in_=vec_ps[:, 0:16])
@@ -175,6 +167,7 @@ def tile_dynamicselfattention_pa_t_kernel(
         acc = {}
         zt = {}
         ysq = {}
+        sq = {}
         ss = {}
         std = {}
         rstd = {}
@@ -186,16 +179,17 @@ def tile_dynamicselfattention_pa_t_kernel(
             if s < 0 or s >= STEPS:
                 return
             unit = s // 2
+            tokens = slice((unit // SIDES) * GROUP_TOKENS, (unit // SIDES + 1) * GROUP_TOKENS)
             for i in range(2):
                 j = (unit % SIDES) * HEADS + 2 * (s % 2) + i
                 w_cols = slice(j * P, (j + 1) * P)
-                acc[s, i] = acc_pool.tile([P, GROUP_TOKENS], F32, name="acc")
+                acc[s, i] = bank_pool.tile([P, GROUP_TOKENS], F32, tag="bank", name="acc")
                 nc.tensor.matmul_mx(
                     out=acc[s, i][:],
                     lhsT=w_codes[:, w_cols].bitcast(FP8X4),
                     lhsT_scale=w_scales[:, w_cols],
-                    rhs=h_codes[unit // SIDES][:].bitcast(FP8X4),
-                    rhs_scale=h_scales[unit // SIDES][:],
+                    rhs=h_codes[:, tokens].bitcast(FP8X4),
+                    rhs_scale=h_scales[:, tokens],
                     start=True,
                     stop=True,
                 )
@@ -228,17 +222,26 @@ def tile_dynamicselfattention_pa_t_kernel(
                 return
             unit = s // 2
             if s % 2 == 0:
-                ss[unit] = ss_pool.tile([P, GROUP], F32, name="ss")
+                sq[unit] = ss_pool.tile([P, GROUP, HEAD], F32, name="sq")
             for i in range(2):
                 t = 2 * (s % 2) + i
                 for head in range(HEADS):
                     nc.tensor.matmul(
-                        out=ss[unit][:, t : t + 1],
+                        out=sq[unit][:, t, :],
                         lhsT=ysq[unit, head][:, t * P : (t + 1) * P],
-                        rhs=ones[:],
+                        rhs=ident[:],
+                        is_transpose=True,
                         start=(head == 0),
                         stop=(head == HEADS - 1),
                     )
+
+        def reduce_squares(unit):
+            if unit < 0 or unit >= UNITS:
+                return
+            ss[unit] = small.tile([P, GROUP], F32, name="ss")
+            nc.vector.tensor_reduce(
+                out=ss[unit][:], in_=sq[unit][:], axis=mybir.AxisListType.X, op=ALU.add
+            )
 
         def root(unit):
             if unit < 0 or unit >= UNITS:
@@ -259,7 +262,7 @@ def tile_dynamicselfattention_pa_t_kernel(
                 return
             unit = s // 2
             t = 2 * (s % 2) + i
-            z[s, i] = z_pool.tile([P, HEADS, HEAD], F32, tag="z", name="z")
+            z[s, i] = bank_pool.tile([P, HEADS, HEAD], F32, tag="bank", name="z")
             for head in range(HEADS):
                 nc.tensor.transpose(
                     z[s, i][:, head, :], zt[unit, head][:, t * P : (t + 1) * P], ident[:]
@@ -308,30 +311,25 @@ def tile_dynamicselfattention_pa_t_kernel(
                 in_=with_cos[unit][:],
             )
 
-        for k in range(-1, STEPS + 5):
-            next_group = k // 4 + 1
-            phase = k % 4
-            prepare = k >= 0 and next_group < GROUPS
-            turn_back(k - 3, 0)
-            sum_squares(k - 2)
-            if prepare and phase < 2:
-                turn_hidden(next_group, phase, turn_pool, "turn")
+        for k in range(-1, STEPS + 6):
             project(k + 1)
+            sum_squares(k - 2)
+            turn_back(k - 3, 0)
             turn_back(k - 3, 1)
+            if k % 2 == 0:
+                reduce_squares((k - 4) // 2)
             scale_and_square(k)
-            if prepare and phase == 1:
-                copy_hidden(next_group, 1)
-            if k % 2 == 1:
-                root((k - 3) // 2)
+            if k % 2 == 0:
+                root((k - 4) // 2)
+            rotate(k - 5)
             if k % 2 == 0:
                 invert((k - 4) // 2)
-            rotate(k - 4)
-            if prepare and phase == 0:
-                copy_hidden(next_group, 0)
-            if prepare and phase == 2:
-                quantise_hidden(next_group)
             if k + 2 < SIDES * HEADS // 2:
                 turn_weights(k + 2)
                 quantise_weights(k + 2)
-            if k % 2 == 0:
-                combine_store((k - 6) // 2)
+            if k + 2 < GROUPS:
+                turn_hidden(k + 2, False)
+            if 1 <= k + 1 < GROUPS:
+                quantise_hidden(k + 1)
+            if k % 2 == 1:
+                combine_store((k - 7) // 2)

@@ -175,12 +175,12 @@ def tile_dynamicselfattention_pa_t_kernel(
         with_cos = {}
         with_sin = {}
 
-        def project(s):
+        def project(s, which):
             if s < 0 or s >= STEPS:
                 return
             unit = s // 2
             tokens = slice((unit // SIDES) * GROUP_TOKENS, (unit // SIDES + 1) * GROUP_TOKENS)
-            for i in range(2):
+            for i in (which,):
                 j = (unit % SIDES) * HEADS + 2 * (s % 2) + i
                 w_cols = slice(j * P, (j + 1) * P)
                 acc[s, i] = bank_pool.tile([P, GROUP_TOKENS], F32, tag="bank", name="acc")
@@ -217,13 +217,13 @@ def tile_dynamicselfattention_pa_t_kernel(
                     bias=bias_col[:, j : j + 1],
                 )
 
-        def sum_squares(s):
+        def sum_squares(s, which):
             if s < 0 or s >= STEPS:
                 return
             unit = s // 2
-            if s % 2 == 0:
+            if s % 2 == 0 and which == 0:
                 sq[unit] = ss_pool.tile([P, GROUP, HEAD], F32, name="sq")
-            for i in range(2):
+            for i in (which,):
                 t = 2 * (s % 2) + i
                 for head in range(HEADS):
                     nc.tensor.matmul(
@@ -312,10 +312,10 @@ def tile_dynamicselfattention_pa_t_kernel(
             )
 
         for k in range(-1, STEPS + 6):
-            project(k + 1)
-            sum_squares(k - 2)
-            turn_back(k - 3, 0)
-            turn_back(k - 3, 1)
+            for i in range(2):
+                project(k + 1, i)
+                sum_squares(k - 2, i)
+                turn_back(k - 3, i)
             if k % 2 == 0:
                 reduce_squares((k - 4) // 2)
             scale_and_square(k)

@@ -175,12 +175,12 @@ def tile_dynamicselfattention_pa_t_kernel(
         with_cos = {}
         with_sin = {}
 
-        def project(s, which):
+        def project(s):
             if s < 0 or s >= STEPS:
                 return
             unit = s // 2
             tokens = slice((unit // SIDES) * GROUP_TOKENS, (unit // SIDES + 1) * GROUP_TOKENS)
-            for i in (which,):
+            for i in range(2):
                 j = (unit % SIDES) * HEADS + 2 * (s % 2) + i
                 w_cols = slice(j * P, (j + 1) * P)
                 acc[s, i] = bank_pool.tile([P, GROUP_TOKENS], F32, tag="bank", name="acc")
@@ -217,13 +217,13 @@ def tile_dynamicselfattention_pa_t_kernel(
                     bias=bias_col[:, j : j + 1],
                 )
 
-        def sum_squares(s, which):
+        def sum_squares(s):
             if s < 0 or s >= STEPS:
                 return
             unit = s // 2
-            if s % 2 == 0 and which == 0:
+            if s % 2 == 0:
                 sq[unit] = ss_pool.tile([P, GROUP, HEAD], F32, name="sq")
-            for i in (which,):
+            for i in range(2):
                 t = 2 * (s % 2) + i
                 for head in range(HEADS):
                     nc.tensor.matmul(
@@ -299,7 +299,7 @@ def tile_dynamicselfattention_pa_t_kernel(
                 in1=s_halves[:, :, 1, :],
                 op=ALU.subtract,
             )
-            nc.gpsimd.tensor_tensor(
+            nc.vector.tensor_tensor(
                 out=c_halves[:, :, 1, :],
                 in0=c_halves[:, :, 1, :],
                 in1=s_halves[:, :, 0, :],
@@ -312,10 +312,10 @@ def tile_dynamicselfattention_pa_t_kernel(
             )
 
         for k in range(-1, STEPS + 6):
-            for i in range(2):
-                project(k + 1, i)
-                sum_squares(k - 2, i)
-                turn_back(k - 3, i)
+            project(k + 1)
+            sum_squares(k - 2)
+            turn_back(k - 3, 0)
+            turn_back(k - 3, 1)
             if k % 2 == 0:
                 reduce_squares((k - 4) // 2)
             scale_and_square(k)

@@ -61,11 +61,12 @@ def tile_dynamicselfattention_pa_t_kernel(
         stack.enter_context(tc.manual_schedule())
         keep = stack.enter_context(tc.tile_pool(name="keep", bufs=1))
         quant = stack.enter_context(tc.tile_pool(name="quant", bufs=2))
-        zt_pool = stack.enter_context(tc.tile_pool(name="zt_pool", bufs=14))
+        zt_pool = stack.enter_context(tc.tile_pool(name="zt_pool", bufs=16))
         ysq_pool = stack.enter_context(tc.tile_pool(name="ysq_pool", bufs=12))
         small = stack.enter_context(tc.tile_pool(name="small", bufs=4))
-        cos_pool = stack.enter_context(tc.tile_pool(name="cos_pool", bufs=4))
-        sin_pool = stack.enter_context(tc.tile_pool(name="sin_pool", bufs=3))
+        cos_pool = stack.enter_context(tc.tile_pool(name="cos_pool", bufs=7))
+        sin_pool = stack.enter_context(tc.tile_pool(name="sin_pool", bufs=6))
+        junk_pool = stack.enter_context(tc.tile_pool(name="junk_pool", bufs=2))
         bank_pool = stack.enter_context(tc.psum_pool(name="bank_pool", bufs=6))
         ss_pool = stack.enter_context(tc.psum_pool(name="ss_pool", bufs=2))
 
@@ -118,11 +119,11 @@ def tile_dynamicselfattention_pa_t_kernel(
         h_scales = keep.tile([P, TOKENS], U8, align_bytes=64)
         h_grouped = {}
 
-        def turn_weights(pair):
+        def turn_weights(pair, on_scalar):
             bank = bank_pool.tile([P, 2, 2, P], F32, tag="bank")
             two = slice(2 * pair, 2 * pair + 2)
             turn_two_blocks(nc, bank, ident[:], w_words[:, two, :])
-            copy_two_blocks(nc, bank, w_grouped_words[:, two], False)
+            copy_two_blocks(nc, bank, w_grouped_words[:, two], on_scalar)
 
         def quantise_weights(pair):
             nc.vector.quantize_mx(
@@ -148,10 +149,6 @@ def tile_dynamicselfattention_pa_t_kernel(
                 out=h_codes[:, tokens].bitcast(FP8X4), scales=h_scales[:, tokens], in_=h_grouped[g][:]
             )
 
-        turn_weights(0)
-        turn_hidden(0, True)
-        quantise_weights(0)
-
         vec_f32 = keep.tile([P, P], F32)
         nc.vector.tensor_copy(out=vec_f32[:], in_=vec_rows[:])
         vec_ps = bank_pool.tile([P, P], F32, tag="bank")
@@ -162,7 +159,15 @@ def tile_dynamicselfattention_pa_t_kernel(
         gain_col = cols[:, 8:16]
         gain_bias = keep.tile([P, 8], F32)
         nc.vector.tensor_mul(out=gain_bias[:], in0=bias_col, in1=gain_col)
+
+        turn_weights(0, False)
+        turn_hidden(0, True)
+        quantise_weights(0)
+        for pair in range(1, SIDES * HEADS // 2):
+            turn_weights(pair, True)
         quantise_hidden(0)
+        for pair in range(1, SIDES * HEADS // 2):
+            quantise_weights(pair)
 
         acc = {}
         zt = {}
@@ -235,13 +240,26 @@ def tile_dynamicselfattention_pa_t_kernel(
                         stop=(head == HEADS - 1),
                     )
 
-        def reduce_squares(unit):
-            if unit < 0 or unit >= UNITS:
+        def reduce_on_vector(unit):
+            if unit < 0 or unit >= UNITS or unit % 2 == 1:
                 return
             ss[unit] = small.tile([P, GROUP], F32, name="ss")
             nc.vector.tensor_reduce(
                 out=ss[unit][:], in_=sq[unit][:], axis=mybir.AxisListType.X, op=ALU.add
             )
+
+        def reduce_on_scalar(unit):
+            if unit < 0 or unit >= UNITS or unit % 2 == 0:
+                return
+            ss[unit] = small.tile([P, GROUP], F32, name="ss")
+            junk = junk_pool.tile([P, GROUP, HEAD], F32)
+            for t in range(GROUP):
+                nc.scalar.activation(
+                    out=junk[:, t, :],
+                    in_=sq[unit][:, t, :],
+                    func=ACT.Identity,
+                    accum_out=ss[unit][:, t : t + 1],
+                )
 
         def root(unit):
             if unit < 0 or unit >= UNITS:
@@ -272,15 +290,14 @@ def tile_dynamicselfattention_pa_t_kernel(
             if s < 0 or s >= STEPS:
                 return
             unit = s // 2
-            if s % 2 == 0:
-                with_cos[unit] = cos_pool.tile([P, GROUP, DIM], F32, name="with_cos")
-                with_sin[unit] = sin_pool.tile([P, GROUP, DIM], F32, name="with_sin")
+            with_cos[s] = cos_pool.tile([P, 2, DIM], F32, name="with_cos")
+            with_sin[s] = sin_pool.tile([P, 2, DIM], F32, name="with_sin")
             for i in range(2):
                 t = 2 * (s % 2) + i
                 T = (unit // SIDES) * GROUP + t
-                for table, product in ((cos_sb, with_cos[unit]), (sin_swap, with_sin[unit])):
+                for table, product in ((cos_sb, with_cos[s]), (sin_swap, with_sin[s])):
                     nc.vector.scalar_tensor_tensor(
-                        out=product[:, t, :].rearrange("p (h d) -> p h d", d=HEAD),
+                        out=product[:, i, :].rearrange("p (h d) -> p h d", d=HEAD),
                         in0=z[s, i][:],
                         scalar=rstd[unit][:, t : t + 1],
                         in1=table[:, T, :].unsqueeze(1).to_broadcast([P, HEADS, HEAD]),
@@ -288,48 +305,46 @@ def tile_dynamicselfattention_pa_t_kernel(
                         op1=ALU.mult,
                     )
 
-        def combine_store(unit):
-            if unit < 0 or unit >= UNITS:
+        def combine_store(s):
+            if s < 0 or s >= STEPS:
                 return
-            c_halves = with_cos[unit][:].rearrange("p t (h x d) -> p (t h) x d", x=2, d=HALF)
-            s_halves = with_sin[unit][:].rearrange("p t (h x d) -> p (t h) x d", x=2, d=HALF)
-            nc.gpsimd.tensor_tensor(
+            engine = nc.vector if s == STEPS - 1 else nc.gpsimd
+            c_halves = with_cos[s][:].rearrange("p t (h x d) -> p (t h) x d", x=2, d=HALF)
+            s_halves = with_sin[s][:].rearrange("p t (h x d) -> p (t h) x d", x=2, d=HALF)
+            engine.tensor_tensor(
                 out=c_halves[:, :, 0, :],
                 in0=c_halves[:, :, 0, :],
                 in1=s_halves[:, :, 1, :],
                 op=ALU.subtract,
             )
-            nc.vector.tensor_tensor(
+            engine.tensor_tensor(
                 out=c_halves[:, :, 1, :],
                 in0=c_halves[:, :, 1, :],
                 in1=s_halves[:, :, 0, :],
                 op=ALU.add,
             )
-            g = unit // SIDES
+            unit = s // 2
+            first = (unit // SIDES) * GROUP + 2 * (s % 2)
             nc.sync.dma_start(
-                out=out_dram[unit % SIDES][:, g * GROUP : (g + 1) * GROUP, :],
-                in_=with_cos[unit][:],
+                out=out_dram[unit % SIDES][:, first : first + 2, :], in_=with_cos[s][:]
             )
 
         for k in range(-1, STEPS + 6):
             project(k + 1)
             sum_squares(k - 2)
-            turn_back(k - 3, 0)
-            turn_back(k - 3, 1)
-            if k % 2 == 0:
-                reduce_squares((k - 4) // 2)
+            turn_back(k - 4, 0)
+            turn_back(k - 4, 1)
             scale_and_square(k)
             if k % 2 == 0:
+                reduce_on_scalar((k - 4) // 2)
                 root((k - 4) // 2)
             rotate(k - 5)
+            if k % 2 == 1:
+                reduce_on_vector((k - 3) // 2)
             if k % 2 == 0:
                 invert((k - 4) // 2)
-            if k + 2 < SIDES * HEADS // 2:
-                turn_weights(k + 2)
-                quantise_weights(k + 2)
             if k + 2 < GROUPS:
                 turn_hidden(k + 2, False)
             if 1 <= k + 1 < GROUPS:
                 quantise_hidden(k + 1)
-            if k % 2 == 1:
-                combine_store((k - 7) // 2)
+            combine_store(k - 6)

from contextlib import ExitStack

import concourse.mybir as mybir
from concourse.masks import make_identity

F32 = mybir.dt.float32
BF16 = mybir.dt.bfloat16
U32 = mybir.dt.uint32
U8 = mybir.dt.uint8
FP8X4 = mybir.dt.float8_e4m3fn_x4
ACT = mybir.ActivationFunctionType
ALU = mybir.AluOpType

P = 128
TOKENS = 4096
DIM = 512
HEAD = 128
HALF = HEAD // 2
HEADS = DIM // HEAD
SIDES = 2
WORDS = DIM // 2
TILES = TOKENS // P
GROUP = 4
GROUPS = TILES // GROUP
GROUP_TOKENS = GROUP * P
UNITS = GROUPS * SIDES
STEPS = 2 * UNITS
EPS = 1e-6

FLOPS = 2 * TOKENS * SIDES * DIM * DIM


def turn_two_blocks(nc, bank, ident, two_blocks):
    for blk in range(2):
        for u in range(2):
            nc.tensor.transpose(bank[:, blk, u, :], two_blocks[:, blk, u * P : (u + 1) * P], ident)


def copy_two_blocks(nc, bank, grouped, on_scalar):
    planes = bank[:].rearrange("p b u r -> p b r u")
    if on_scalar:
        nc.scalar.copy(out=grouped, in_=planes)
    else:
        nc.vector.tensor_copy(out=grouped, in_=planes)


def tile_dynamicselfattention_pa_t_kernel(
    tc, hidden_states, cos, sin, w_qk, b_qk, g_q, g_k, out_0, out_1
):
    nc = tc.nc
    h_dram = hidden_states.flatten_outer_dims().rearrange("(p T) k -> p T k", T=TILES)
    cos_dram = cos.rearrange("(p T) d -> p T d", T=TILES)
    sin_dram = sin.rearrange("(p T) d -> p T d", T=TILES)
    w_dram = w_qk.rearrange("(j p) k -> p j k", p=P)
    out_dram = [
        o.flatten_outer_dims().rearrange("(p T h) d -> p T (h d)", T=TILES, h=HEADS)
        for o in (out_0, out_1)
    ]

    with ExitStack() as stack:
        stack.enter_context(tc.manual_schedule())
        keep = stack.enter_context(tc.tile_pool(name="keep", bufs=1))
        quant = stack.enter_context(tc.tile_pool(name="quant", bufs=2))
        zt_pool = stack.enter_context(tc.tile_pool(name="zt_pool", bufs=16))
        ysq_pool = stack.enter_context(tc.tile_pool(name="ysq_pool", bufs=12))
        small = stack.enter_context(tc.tile_pool(name="small", bufs=4))
        cos_pool = stack.enter_context(tc.tile_pool(name="cos_pool", bufs=7))
        sin_pool = stack.enter_context(tc.tile_pool(name="sin_pool", bufs=6))
        junk_pool = stack.enter_context(tc.tile_pool(name="junk_pool", bufs=2))
        bank_pool = stack.enter_context(tc.psum_pool(name="bank_pool", bufs=6))
        ss_pool = stack.enter_context(tc.psum_pool(name="ss_pool", bufs=2))

        eps = keep.tile([P, 1], F32)
        nc.vector.memset(eps[:], EPS)
        warm = keep.tile([P, 1], F32)
        nc.scalar.activation(out=warm[:], in_=eps[:], func=ACT.Sqrt)
        vec_rows = keep.tile([P, P], BF16)
        nc.vector.memset(vec_rows[:], 0.0)
        ident = keep.tile([P, P], F32)
        make_identity(nc, ident[:])

        w_sb = keep.tile([P, SIDES * HEADS * DIM], BF16)
        w_rows = w_sb[:].rearrange("p (j k) -> p j k", k=DIM)
        h_sb = keep.tile([P, TILES * DIM], BF16)
        h_rows = h_sb[:].rearrange("p (T k) -> p T k", k=DIM)

        def load_w(pair):
            two = slice(2 * pair, 2 * pair + 2)
            nc.sync.dma_start(out=w_rows[:, two, :], in_=w_dram[:, two, :])

        def load_h(g):
            four = slice(g * GROUP, (g + 1) * GROUP)
            nc.sync.dma_start(out=h_rows[:, four, :], in_=h_dram[:, four, :])

        nc.scalar.dma_start(out=vec_rows[0:8, :], in_=b_qk.rearrange("(j d) -> j d", d=HEAD))
        nc.scalar.dma_start(out=vec_rows[8:12, :], in_=g_q.rearrange("(j d) -> j d", d=HEAD))
        nc.scalar.dma_start(out=vec_rows[12:16, :], in_=g_k.rearrange("(j d) -> j d", d=HEAD))
        load_w(0)
        load_h(0)
        for pair in range(1, SIDES * HEADS // 2):
            load_w(pair)
        cos_sb = keep.tile([P, TILES, HEAD], BF16)
        sin_swap = keep.tile([P, TILES, HEAD], BF16)
        for part in range(2):
            for g in range(max(1, part * GROUPS // 2), (part + 1) * GROUPS // 2):
                load_h(g)
            some = slice(part * TILES // 2, (part + 1) * TILES // 2)
            nc.sync.dma_start(out=cos_sb[:, some, :], in_=cos_dram[:, some, :])
            nc.sync.dma_start(out=sin_swap[:, some, 0:HALF], in_=sin_dram[:, some, HALF:HEAD])
            nc.sync.dma_start(out=sin_swap[:, some, HALF:HEAD], in_=sin_dram[:, some, 0:HALF])

        w_words = w_sb[:].bitcast(F32).rearrange("p (j w) -> p j w", w=WORDS)
        h_words = h_sb[:].bitcast(F32).rearrange("p (T w) -> p T w", w=WORDS)
        w_grouped = keep.tile([P, SIDES * DIM * 4], BF16, align_bytes=64)
        w_grouped_words = w_grouped[:].bitcast(F32).rearrange("p (j r u) -> p j r u", r=P, u=2)
        w_codes = keep.tile([P, SIDES * DIM], U32, align_bytes=64)
        w_scales = keep.tile([P, SIDES * DIM], U8, align_bytes=64)
        h_codes = keep.tile([P, TOKENS], U32, align_bytes=64)
        h_scales = keep.tile([P, TOKENS], U8, align_bytes=64)
        h_grouped = {}

        def turn_weights(pair, on_scalar):
            bank = bank_pool.tile([P, 2, 2, P], F32, tag="bank")
            two = slice(2 * pair, 2 * pair + 2)
            turn_two_blocks(nc, bank, ident[:], w_words[:, two, :])
            copy_two_blocks(nc, bank, w_grouped_words[:, two], on_scalar)

        def quantise_weights(pair):
            nc.vector.quantize_mx(
                out=w_codes[:, 2 * P * pair : 2 * P * (pair + 1)].bitcast(FP8X4),
                scales=w_scales[:, 2 * P * pair : 2 * P * (pair + 1)],
                in_=w_grouped[:, 8 * P * pair : 8 * P * (pair + 1)],
            )

        def turn_hidden(g, second_on_scalar):
            h_grouped[g] = quant.tile([P, GROUP_TOKENS * 4], BF16, align_bytes=64, name="h_grouped")
            words = h_grouped[g][:].bitcast(F32).rearrange("p (t r u) -> p t r u", r=P, u=2)
            for pair in range(GROUP // 2):
                first = g * GROUP + 2 * pair
                bank = bank_pool.tile([P, 2, 2, P], F32, tag="bank")
                turn_two_blocks(nc, bank, ident[:], h_words[:, first : first + 2, :])
                copy_two_blocks(
                    nc, bank, words[:, 2 * pair : 2 * pair + 2], second_on_scalar and pair == 1
                )

        def quantise_hidden(g):
            tokens = slice(g * GROUP_TOKENS, (g + 1) * GROUP_TOKENS)
            nc.vector.quantize_mx(
                out=h_codes[:, tokens].bitcast(FP8X4), scales=h_scales[:, tokens], in_=h_grouped[g][:]
            )

        vec_f32 = keep.tile([P, P], F32)
        nc.vector.tensor_copy(out=vec_f32[:], in_=vec_rows[:])
        vec_ps = bank_pool.tile([P, P], F32, tag="bank")
        nc.tensor.transpose(vec_ps[:], vec_f32[:], ident[:])
        cols = keep.tile([P, 16], F32)
        nc.vector.tensor_copy(out=cols[:], in_=vec_ps[:, 0:16])
        bias_col = cols[:, 0:8]
        gain_col = cols[:, 8:16]
        gain_bias = keep.tile([P, 8], F32)
        nc.vector.tensor_mul(out=gain_bias[:], in0=bias_col, in1=gain_col)

        turn_weights(0, False)
        turn_hidden(0, True)
        quantise_weights(0)
        for pair in range(1, SIDES * HEADS // 2):
            turn_weights(pair, True)
        quantise_hidden(0)
        for pair in range(1, SIDES * HEADS // 2):
            quantise_weights(pair)

        acc = {}
        zt = {}
        ysq = {}
        sq = {}
        ss = {}
        std = {}
        rstd = {}
        z = {}
        with_cos = {}
        with_sin = {}

        def project(s):
            if s < 0 or s >= STEPS:
                return
            unit = s // 2
            tokens = slice((unit // SIDES) * GROUP_TOKENS, (unit // SIDES + 1) * GROUP_TOKENS)
            for i in range(2):
                j = (unit % SIDES) * HEADS + 2 * (s % 2) + i
                w_cols = slice(j * P, (j + 1) * P)
                acc[s, i] = bank_pool.tile([P, GROUP_TOKENS], F32, tag="bank", name="acc")
                nc.tensor.matmul_mx(
                    out=acc[s, i][:],
                    lhsT=w_codes[:, w_cols].bitcast(FP8X4),
                    lhsT_scale=w_scales[:, w_cols],
                    rhs=h_codes[:, tokens].bitcast(FP8X4),
                    rhs_scale=h_scales[:, tokens],
                    start=True,
                    stop=True,
                )

        def scale_and_square(s):
            if s < 0 or s >= STEPS:
                return
            unit = s // 2
            for i in range(2):
                head = 2 * (s % 2) + i
                j = (unit % SIDES) * HEADS + head
                zt[unit, head] = zt_pool.tile([P, GROUP_TOKENS], F32, name="zt")
                nc.scalar.activation(
                    out=zt[unit, head][:],
                    in_=acc[s, i][:],
                    func=ACT.Identity,
                    bias=gain_bias[:, j : j + 1],
                    scale=gain_col[:, j : j + 1],
                )
                ysq[unit, head] = ysq_pool.tile([P, GROUP_TOKENS], F32, name="ysq")
                nc.scalar.activation(
                    out=ysq[unit, head][:],
                    in_=acc[s, i][:],
                    func=ACT.Square,
                    bias=bias_col[:, j : j + 1],
                )

        def sum_squares(s):
            if s < 0 or s >= STEPS:
                return
            unit = s // 2
            if s % 2 == 0:
                sq[unit] = ss_pool.tile([P, GROUP, HEAD], F32, name="sq")
            for i in range(2):
                t = 2 * (s % 2) + i
                for head in range(HEADS):
                    nc.tensor.matmul(
                        out=sq[unit][:, t, :],
                        lhsT=ysq[unit, head][:, t * P : (t + 1) * P],
                        rhs=ident[:],
                        is_transpose=True,
                        start=(head == 0),
                        stop=(head == HEADS - 1),
                    )

        def reduce_on_vector(unit):
            if unit < 0 or unit >= UNITS or unit % 2 == 1:
                return
            ss[unit] = small.tile([P, GROUP], F32, name="ss")
            nc.vector.tensor_reduce(
                out=ss[unit][:], in_=sq[unit][:], axis=mybir.AxisListType.X, op=ALU.add
            )

        def reduce_on_scalar(unit):
            if unit < 0 or unit >= UNITS or unit % 2 == 0:
                return
            ss[unit] = small.tile([P, GROUP], F32, name="ss")
            junk = junk_pool.tile([P, GROUP, HEAD], F32)
            for t in range(GROUP):
                nc.scalar.activation(
                    out=junk[:, t, :],
                    in_=sq[unit][:, t, :],
                    func=ACT.Identity,
                    accum_out=ss[unit][:, t : t + 1],
                )

        def root(unit):
            if unit < 0 or unit >= UNITS:
                return
            std[unit] = small.tile([P, GROUP], F32, name="std")
            nc.scalar.activation(
                out=std[unit][:], in_=ss[unit][:], func=ACT.Sqrt, bias=eps[:], scale=1.0 / DIM
            )

        def invert(unit):
            if unit < 0 or unit >= UNITS:
                return
            rstd[unit] = small.tile([P, GROUP], F32, name="rstd")
            nc.vector.reciprocal(out=rstd[unit][:], in_=std[unit][:])

        def turn_back(s, i):
            if s < 0 or s >= STEPS:
                return
            unit = s // 2
            t = 2 * (s % 2) + i
            z[s, i] = bank_pool.tile([P, HEADS, HEAD], F32, tag="bank", name="z")
            for head in range(HEADS):
                nc.tensor.transpose(
                    z[s, i][:, head, :], zt[unit, head][:, t * P : (t + 1) * P], ident[:]
                )

        def rotate(s):
            if s < 0 or s >= STEPS:
                return
            unit = s // 2
            with_cos[s] = cos_pool.tile([P, 2, DIM], F32, name="with_cos")
            with_sin[s] = sin_pool.tile([P, 2, DIM], F32, name="with_sin")
            for i in range(2):
                t = 2 * (s % 2) + i
                T = (unit // SIDES) * GROUP + t
                for table, product in ((cos_sb, with_cos[s]), (sin_swap, with_sin[s])):
                    nc.vector.scalar_tensor_tensor(
                        out=product[:, i, :].rearrange("p (h d) -> p h d", d=HEAD),
                        in0=z[s, i][:],
                        scalar=rstd[unit][:, t : t + 1],
                        in1=table[:, T, :].unsqueeze(1).to_broadcast([P, HEADS, HEAD]),
                        op0=ALU.mult,
                        op1=ALU.mult,
                    )

        def combine_store(s):
            if s < 0 or s >= STEPS:
                return
            engine = nc.vector if s == STEPS - 1 else nc.gpsimd
            c_halves = with_cos[s][:].rearrange("p t (h x d) -> p (t h) x d", x=2, d=HALF)
            s_halves = with_sin[s][:].rearrange("p t (h x d) -> p (t h) x d", x=2, d=HALF)
            engine.tensor_tensor(
                out=c_halves[:, :, 0, :],
                in0=c_halves[:, :, 0, :],
                in1=s_halves[:, :, 1, :],
                op=ALU.subtract,
            )
            engine.tensor_tensor(
                out=c_halves[:, :, 1, :],
                in0=c_halves[:, :, 1, :],
                in1=s_halves[:, :, 0, :],
                op=ALU.add,
            )
            unit = s // 2
            first = (unit // SIDES) * GROUP + 2 * (s % 2)
            nc.sync.dma_start(
                out=out_dram[unit % SIDES][:, first : first + 2, :], in_=with_cos[s][:]
            )

        for k in range(-1, STEPS + 6):
            project(k + 1)
            sum_squares(k - 2)
            turn_back(k - 4, 0)
            turn_back(k - 4, 1)
            scale_and_square(k)
            if k % 2 == 0:
                reduce_on_scalar((k - 4) // 2)
                root((k - 4) // 2)
            rotate(k - 5)
            if k % 2 == 1:
                reduce_on_vector((k - 3) // 2)
            if k % 2 == 0:
                invert((k - 4) // 2)
            if k + 2 < GROUPS:
                turn_hidden(k + 2, False)
            if 1 <= k + 1 < GROUPS:
                quantise_hidden(k + 1)
            combine_store(k - 6)
